import numpy as np
import ml_dtypes


def mxq(x, axis, fmt="e4m3"):
    dtype, down = {"e4m3": (ml_dtypes.float8_e4m3fn, 7), "e5m2": (ml_dtypes.float8_e5m2, 14)}[fmt]
    v = np.moveaxis(np.asarray(x, np.float32).astype(ml_dtypes.bfloat16).astype(np.float64), axis, -1)
    blocks = v.reshape(v.shape[:-1] + (-1, 32))
    amax = np.abs(blocks).max(-1, keepdims=True)
    byte = np.maximum(np.where(amax > 0, np.frexp(amax)[1] - 1 + 127, 0) - down, 1)
    scale = np.exp2(byte - 127.0)
    codes = (blocks / scale).astype(np.float32).astype(dtype).astype(np.float64)
    return np.moveaxis((codes * scale).reshape(v.shape), -1, axis)


WIDE = False


def mx_kscale(k):
    if not WIDE:
        return np.ones(k)
    levels = np.array([10, -10, 5, -5, 0])
    if k % 512:
        return np.exp2(np.random.permutation(np.resize(levels, k // 32))).repeat(32)
    a = np.empty((k // 512, 16))
    for p in range(k // 512):
        a[p, :8] = np.random.permutation(np.resize(levels, 8))
        for g in range(8):
            far = levels[np.abs(levels - a[p, g]) >= 10]
            a[p, g + 8] = far[np.random.randint(len(far))]
    return np.exp2(a.ravel()).repeat(32)


BF16 = ml_dtypes.bfloat16


def bf(x):
    return np.asarray(x, np.float32).astype(BF16)


def f64(x):
    return np.asarray(x).astype(np.float64)


B, L, C, KS, NL, BH, R = 1, 128, 512, 4, 24, 64, 4
OUT = 2 * BH * NL


def setup_inputs():
    s, t = mx_kscale(C), mx_kscale(C)
    return {"local_features": bf(np.random.standard_normal((B, L, C)) * s),
            "wt": bf(np.random.standard_normal((C, C, KS)) / np.sqrt(C) / s[:, None, None] * t[None, :, None]),
            "bt": bf(np.random.standard_normal(C) * 0.5 * t),
            "w1": bf(np.random.standard_normal((OUT, C)) / np.sqrt(C) / t[None, :]),
            "b1": bf(np.random.standard_normal(OUT) * 0.5)}


def reference(local_features, wt, bt, w1, b1):
    xq = mxq(f64(local_features), 2, "e4m3")
    wq = mxq(f64(wt), 0, "e4m3")
    up = xq @ wq.reshape(C, C * KS)
    up = up.reshape(B, L, C, KS).transpose(0, 2, 1, 3).reshape(B, C, L * KS) + f64(bt)[None, :, None]
    y = (mxq(f64(w1), 1, "e4m3") @ mxq(up, 1, "e4m3")) + f64(b1)[None, :, None]
    y = np.tile(y, (1, 1, R))
    y = y.reshape(B, NL, 2 * BH, L * KS * R)
    return np.ascontiguousarray(y.transpose(2, 0, 1, 3))

@@ -1,0 +1,224 @@
+from contextlib import ExitStack
+
+import concourse.mybir as mybir
+from concourse.masks import make_identity
+
+BF16 = mybir.dt.bfloat16
+F32 = mybir.dt.float32
+U32 = mybir.dt.uint32
+U8 = mybir.dt.uint8
+FP8X4 = mybir.dt.float8_e4m3fn_x4
+ADD = mybir.AluOpType.add
+IDENTITY = mybir.ActivationFunctionType.Identity
+
+P = 128
+PACK = 4
+HALVES = 2
+L = 128
+C = 512
+TAPS = 4
+T = L * TAPS
+LAYERS = 24
+REPEATS = 4
+WT_COLS = C * TAPS
+PIECES = 4
+W1_ROWS = 4
+GROUP = W1_ROWS
+GROUPS = LAYERS // GROUP
+STORE = 2
+
+FLOPS = 2 * L * C * WT_COLS + 2 * LAYERS * P * C * T
+
+
+def tile_conditionalfeaturesupsample_kernel(tc, local_features, wt, bt, w1, b1, out):
+    nc = tc.nc
+    with ExitStack() as ctx:
+        keep = ctx.enter_context(tc.tile_pool(name="keep", bufs=1))
+        stage = ctx.enter_context(tc.tile_pool(name="stage", bufs=2))
+        results = ctx.enter_context(tc.tile_pool(name="results", bufs=4))
+        word_banks = ctx.enter_context(tc.psum_pool(name="word_banks", bufs=3))
+        sum_banks = ctx.enter_context(tc.psum_pool(name="sum_banks", bufs=5))
+
+        ident = keep.tile([P, P], F32)
+        make_identity(nc, ident[:])
+
+        x_rows = keep.tile([P, C], BF16)
+        nc.sync.dma_start(out=x_rows[:], in_=local_features.rearrange("b l c -> (b l) c"))
+
+        wt_rows = keep.tile([P, PACK, WT_COLS], BF16)
+        wt_matrix = wt.rearrange("c o k -> c (o k)")
+        piece_cols = WT_COLS // PIECES
+        for piece in range(PIECES):
+            cols = slice(piece * piece_cols, (piece + 1) * piece_cols)
+            nc.sync.dma_start(
+                out=wt_rows[:, :, cols],
+                in_=wt_matrix[:, cols].rearrange("(p j) w -> p j w", j=PACK),
+            )
+
+        w1_rows = keep.tile([P, GROUPS, W1_ROWS, C], BF16)
+        for g in range(GROUPS):
+            nc.sync.dma_start(
+                out=w1_rows[:, g],
+                in_=w1[g * GROUP * P : (g + 1) * GROUP * P, :].rearrange(
+                    "(q s) c -> q s c", s=W1_ROWS
+                ),
+            )
+
+        bias_rows = keep.tile([P, P], F32)
+        nc.vector.memset(bias_rows[:], 0.0)
+        b1_rows = keep.tile([LAYERS, P], BF16)
+        nc.scalar.dma_start(out=b1_rows[:], in_=b1.rearrange("(n j) -> n j", j=P))
+        bt_rows = keep.tile([P, PACK], BF16)
+        nc.scalar.dma_start(out=bt_rows[:], in_=bt.rearrange("(p t) -> p t", t=PACK))
+
+        x_bank = word_banks.tile([P, T], F32, tag="words")
+        for u in range(HALVES):
+            nc.tensor.transpose(
+                x_bank[:, u * P : (u + 1) * P], x_rows[:].bitcast(F32)[:, u : HALVES * P : HALVES], ident[:]
+            )
+        x_grouped = keep.tile([P, L * PACK], BF16, align_bytes=64)
+        nc.vector.tensor_copy(
+            out=x_grouped[:].bitcast(F32).rearrange("p (l u) -> p l u", u=HALVES),
+            in_=x_bank[:, 0 : HALVES * P].rearrange("p (u l) -> p l u", u=HALVES),
+        )
+        nc.vector.tensor_copy(out=bias_rows[0:LAYERS, :], in_=b1_rows[:])
+        x_codes = keep.tile([P, L], U32, align_bytes=64)
+        x_scales = keep.tile([P, L], U8, align_bytes=64)
+        nc.vector.quantize_mx(out=x_codes[:].bitcast(FP8X4), scales=x_scales[:], in_=x_grouped[:])
+
+        bias_bank = word_banks.tile([P, T], F32, tag="words")
+        nc.tensor.transpose(bias_bank[:, 0:P], bias_rows[:], ident[:])
+        b1_col = keep.tile([P, LAYERS], F32)
+        nc.vector.tensor_copy(out=b1_col[:], in_=bias_bank[:, 0:LAYERS])
+        bt_col = keep.tile([P, PACK], F32)
+        nc.vector.tensor_copy(out=bt_col[:], in_=bt_rows[:])
+
+        wt_grouped = keep.tile([P, PACK, TAPS, P, PACK], BF16, align_bytes=64)
+        wt_codes = keep.tile([P, PACK, TAPS, P], U32, align_bytes=64)
+        wt_scales = keep.tile([P, PACK, TAPS, P], U8, align_bytes=64)
+        wt_sorted = wt_rows[:].rearrange("p j (m t k) -> p t m j k", t=PACK, k=TAPS)
+        wt_targets = wt_grouped[:].rearrange("p t k m j -> p t m j k")
+        up_banks = []
+        for k in range(TAPS):
+            up_bank = sum_banks.tile([P, T], F32, tag="sums")
+            up_banks.append(up_bank)
+
+        def wt_copies(piece):
+            ms = slice(piece * P // PIECES, (piece + 1) * P // PIECES)
+            for t in range(PACK // 2):
+                nc.vector.tensor_copy(out=wt_targets[:, t, ms], in_=wt_sorted[:, t, ms])
+                nc.scalar.copy(out=wt_targets[:, t + 2, ms], in_=wt_sorted[:, t + 2, ms])
+
+        def wt_products():
+            for t in range(PACK):
+                for k in range(TAPS):
+                    nc.vector.quantize_mx(
+                        out=wt_codes[:, t, k].bitcast(FP8X4),
+                        scales=wt_scales[:, t, k],
+                        in_=wt_grouped[:, t, k].rearrange("p m j -> p (m j)"),
+                    )
+                    nc.tensor.matmul_mx(
+                        out=up_banks[k][:, t * L : (t + 1) * L],
+                        lhsT=wt_codes[:, t, k].bitcast(FP8X4),
+                        lhsT_scale=wt_scales[:, t, k],
+                        rhs=x_codes[:].bitcast(FP8X4),
+                        rhs_scale=x_scales[:],
+                        start=True,
+                        stop=True,
+                    )
+
+        w1_codes = keep.tile([P, LAYERS, P], U32, align_bytes=64)
+        w1_scales = keep.tile([P, LAYERS, P], U8, align_bytes=64)
+
+        per_bank = T // P
+
+        def w1_transposes(g):
+            w1_banks = []
+            for first in range(0, W1_ROWS * HALVES, per_bank):
+                w1_bank = word_banks.tile([P, T], F32, tag="words")
+                for f in range(per_bank):
+                    s, u = divmod(first + f, HALVES)
+                    nc.tensor.transpose(
+                        w1_bank[:, f * P : (f + 1) * P],
+                        w1_rows[:, g, s].bitcast(F32)[:, u : HALVES * P : HALVES],
+                        ident[:],
+                    )
+                w1_banks.append(w1_bank)
+            return w1_banks
+
+        def w1_copies(w1_banks):
+            w1_grouped = stage.tile([P, GROUP * P * PACK], BF16, align_bytes=64)
+            words = w1_grouped[:].bitcast(F32).rearrange("p (q f) -> p q f", f=W1_ROWS * HALVES)
+            for b in range(len(w1_banks)):
+                nc.scalar.copy(
+                    out=words[:, :, b * per_bank : (b + 1) * per_bank],
+                    in_=w1_banks[b][:].rearrange("p (f q) -> p q f", f=per_bank),
+                )
+            return w1_grouped
+
+        def w1_quantise(g, w1_grouped):
+            layers = slice(g * GROUP, (g + 1) * GROUP)
+            nc.vector.quantize_mx(
+                out=w1_codes[:, layers].rearrange("p n j -> p (n j)").bitcast(FP8X4),
+                scales=w1_scales[:, layers].rearrange("p n j -> p (n j)"),
+                in_=w1_grouped[:],
+            )
+
+        for piece in range(PIECES):
+            wt_copies(piece)
+        w1_banks = w1_transposes(0)
+        wt_products()
+        w1_grouped = w1_copies(w1_banks)
+
+        up_grouped = keep.tile([P, TAPS, L, PACK], BF16, align_bytes=64)
+        for k in range(TAPS):
+            nc.vector.tensor_tensor(
+                out=up_grouped[:, k],
+                in0=up_banks[k][:].rearrange("p (j l) -> p l j", j=PACK),
+                in1=bt_col[:].unsqueeze(1).to_broadcast([P, L, PACK]),
+                op=ADD,
+            )
+        w1_quantise(0, w1_grouped)
+        up_codes = keep.tile([P, T], U32, align_bytes=64)
+        up_scales = keep.tile([P, T], U8, align_bytes=64)
+        nc.vector.quantize_mx(
+            out=up_codes[:].bitcast(FP8X4),
+            scales=up_scales[:],
+            in_=up_grouped[:].rearrange("p k l j -> p (k l j)"),
+        )
+
+        for g in range(GROUPS):
+            for first in range(g * GROUP, (g + 1) * GROUP, STORE):
+                y_rows = results.tile([P, STORE, REPEATS * T], F32)
+                for i in range(STORE):
+                    n = first + i
+                    y_bank = sum_banks.tile([P, T], F32, tag="sums")
+                    nc.tensor.matmul_mx(
+                        out=y_bank[:],
+                        lhsT=w1_codes[:, n].bitcast(FP8X4),
+                        lhsT_scale=w1_scales[:, n],
+                        rhs=up_codes[:].bitcast(FP8X4),
+                        rhs_scale=up_scales[:],
+                        start=True,
+                        stop=True,
+                    )
+                    repeated = (
+                        y_bank[:]
+                        .rearrange("p (k l) -> p l k", k=TAPS)
+                        .unsqueeze(1)
+                        .to_broadcast([P, REPEATS, L, TAPS])
+                    )
+                    target = y_rows[:, i].rearrange("p (r l k) -> p r l k", r=REPEATS, k=TAPS)
+                    if i % 2 == 0:
+                        nc.scalar.activation(
+                            out=target, in_=repeated, func=IDENTITY, bias=b1_col[:, n : n + 1]
+                        )
+                    else:
+                        nc.vector.tensor_scalar(
+                            out=target, in0=repeated, scalar1=b1_col[:, n : n + 1], scalar2=None, op0=ADD
+                        )
+                nc.sync.dma_start(out=out[:, 0, first : first + STORE, :], in_=y_rows[:])
+                if first == g * GROUP and g + 1 < GROUPS:
+                    w1_grouped = w1_copies(w1_transposes(g + 1))
+            if g + 1 < GROUPS:
+                w1_quantise(g + 1, w1_grouped)

@@ -1,4 +1,5 @@
 from contextlib import ExitStack
+from functools import partial
 
 import concourse.mybir as mybir
 from concourse.masks import make_identity
@@ -21,10 +22,10 @@ T = L * TAPS
 LAYERS = 24
 REPEATS = 4
 WT_COLS = C * TAPS
-PIECES = 4
-W1_ROWS = 4
-GROUP = W1_ROWS
-GROUPS = LAYERS // GROUP
+PIECES = ((0, 64), (64, 96), (96, 128))
+HALF = P // 2
+GROUPS = (2, 2, 4, 4, 4, 4, 4)
+ONCE = 2
 STORE = 2
 
 FLOPS = 2 * L * C * WT_COLS + 2 * LAYERS * P * C * T
@@ -42,34 +43,35 @@ def tile_conditionalfeaturesupsample_kernel(tc, local_features, wt, bt, w1, b1, 
         ident = keep.tile([P, P], F32)
         make_identity(nc, ident[:])
 
+        bias_rows = keep.tile([P, P], F32)
+        nc.vector.memset(bias_rows[:], 0.0)
+        b1_rows = keep.tile([LAYERS, P], BF16)
+        bt_rows = keep.tile([P, PACK], BF16)
+
         x_rows = keep.tile([P, C], BF16)
         nc.sync.dma_start(out=x_rows[:], in_=local_features.rearrange("b l c -> (b l) c"))
 
         wt_rows = keep.tile([P, PACK, WT_COLS], BF16)
         wt_matrix = wt.rearrange("c o k -> c (o k)")
-        piece_cols = WT_COLS // PIECES
-        for piece in range(PIECES):
-            cols = slice(piece * piece_cols, (piece + 1) * piece_cols)
+        m_cols = WT_COLS // P
+        for m0, m1 in PIECES:
+            cols = slice(m0 * m_cols, m1 * m_cols)
             nc.sync.dma_start(
                 out=wt_rows[:, :, cols],
                 in_=wt_matrix[:, cols].rearrange("(p j) w -> p j w", j=PACK),
             )
+            if m0 == 0:
+                nc.sync.dma_start(out=bt_rows[:], in_=bt.rearrange("(p t) -> p t", t=PACK))
+                nc.sync.dma_start(out=b1_rows[:], in_=b1.rearrange("(n j) -> n j", j=P))
 
-        w1_rows = keep.tile([P, GROUPS, W1_ROWS, C], BF16)
-        for g in range(GROUPS):
+        w1_rows = keep.tile([P, LAYERS, C], BF16)
+        n0 = 0
+        for layers in GROUPS:
             nc.sync.dma_start(
-                out=w1_rows[:, g],
-                in_=w1[g * GROUP * P : (g + 1) * GROUP * P, :].rearrange(
-                    "(q s) c -> q s c", s=W1_ROWS
-                ),
+                out=w1_rows[:, n0 : n0 + layers],
+                in_=w1[n0 * P : (n0 + layers) * P, :].rearrange("(q s) c -> q s c", s=layers),
             )
-
-        bias_rows = keep.tile([P, P], F32)
-        nc.vector.memset(bias_rows[:], 0.0)
-        b1_rows = keep.tile([LAYERS, P], BF16)
-        nc.scalar.dma_start(out=b1_rows[:], in_=b1.rearrange("(n j) -> n j", j=P))
-        bt_rows = keep.tile([P, PACK], BF16)
-        nc.scalar.dma_start(out=bt_rows[:], in_=bt.rearrange("(p t) -> p t", t=PACK))
+            n0 += layers
 
         x_bank = word_banks.tile([P, T], F32, tag="words")
         for u in range(HALVES):
@@ -81,17 +83,9 @@ def tile_conditionalfeaturesupsample_kernel(tc, local_features, wt, bt, w1, b1, 
             out=x_grouped[:].bitcast(F32).rearrange("p (l u) -> p l u", u=HALVES),
             in_=x_bank[:, 0 : HALVES * P].rearrange("p (u l) -> p l u", u=HALVES),
         )
-        nc.vector.tensor_copy(out=bias_rows[0:LAYERS, :], in_=b1_rows[:])
         x_codes = keep.tile([P, L], U32, align_bytes=64)
         x_scales = keep.tile([P, L], U8, align_bytes=64)
         nc.vector.quantize_mx(out=x_codes[:].bitcast(FP8X4), scales=x_scales[:], in_=x_grouped[:])
-
-        bias_bank = word_banks.tile([P, T], F32, tag="words")
-        nc.tensor.transpose(bias_bank[:, 0:P], bias_rows[:], ident[:])
-        b1_col = keep.tile([P, LAYERS], F32)
-        nc.vector.tensor_copy(out=b1_col[:], in_=bias_bank[:, 0:LAYERS])
-        bt_col = keep.tile([P, PACK], F32)
-        nc.vector.tensor_copy(out=bt_col[:], in_=bt_rows[:])
 
         wt_grouped = keep.tile([P, PACK, TAPS, P, PACK], BF16, align_bytes=64)
         wt_codes = keep.tile([P, PACK, TAPS, P], U32, align_bytes=64)
@@ -104,121 +98,161 @@ def tile_conditionalfeaturesupsample_kernel(tc, local_features, wt, bt, w1, b1, 
             up_banks.append(up_bank)
 
         def wt_copies(piece):
-            ms = slice(piece * P // PIECES, (piece + 1) * P // PIECES)
+            ms = slice(piece[0], piece[1])
             for t in range(PACK // 2):
                 nc.vector.tensor_copy(out=wt_targets[:, t, ms], in_=wt_sorted[:, t, ms])
                 nc.scalar.copy(out=wt_targets[:, t + 2, ms], in_=wt_sorted[:, t + 2, ms])
 
-        def wt_products():
-            for t in range(PACK):
-                for k in range(TAPS):
-                    nc.vector.quantize_mx(
-                        out=wt_codes[:, t, k].bitcast(FP8X4),
-                        scales=wt_scales[:, t, k],
-                        in_=wt_grouped[:, t, k].rearrange("p m j -> p (m j)"),
-                    )
-                    nc.tensor.matmul_mx(
-                        out=up_banks[k][:, t * L : (t + 1) * L],
-                        lhsT=wt_codes[:, t, k].bitcast(FP8X4),
-                        lhsT_scale=wt_scales[:, t, k],
-                        rhs=x_codes[:].bitcast(FP8X4),
-                        rhs_scale=x_scales[:],
-                        start=True,
-                        stop=True,
-                    )
-
-        w1_codes = keep.tile([P, LAYERS, P], U32, align_bytes=64)
-        w1_scales = keep.tile([P, LAYERS, P], U8, align_bytes=64)
-
-        per_bank = T // P
-
-        def w1_transposes(g):
-            w1_banks = []
-            for first in range(0, W1_ROWS * HALVES, per_bank):
-                w1_bank = word_banks.tile([P, T], F32, tag="words")
-                for f in range(per_bank):
-                    s, u = divmod(first + f, HALVES)
-                    nc.tensor.transpose(
-                        w1_bank[:, f * P : (f + 1) * P],
-                        w1_rows[:, g, s].bitcast(F32)[:, u : HALVES * P : HALVES],
-                        ident[:],
-                    )
-                w1_banks.append(w1_bank)
-            return w1_banks
-
-        def w1_copies(w1_banks):
-            w1_grouped = stage.tile([P, GROUP * P * PACK], BF16, align_bytes=64)
-            words = w1_grouped[:].bitcast(F32).rearrange("p (q f) -> p q f", f=W1_ROWS * HALVES)
-            for b in range(len(w1_banks)):
-                nc.scalar.copy(
-                    out=words[:, :, b * per_bank : (b + 1) * per_bank],
-                    in_=w1_banks[b][:].rearrange("p (f q) -> p q f", f=per_bank),
-                )
-            return w1_grouped
-
-        def w1_quantise(g, w1_grouped):
-            layers = slice(g * GROUP, (g + 1) * GROUP)
+        def wt_quantise(h, t, k):
+            ms = slice(h * HALF, (h + 1) * HALF)
             nc.vector.quantize_mx(
-                out=w1_codes[:, layers].rearrange("p n j -> p (n j)").bitcast(FP8X4),
-                scales=w1_scales[:, layers].rearrange("p n j -> p (n j)"),
-                in_=w1_grouped[:],
+                out=wt_codes[:, t, k, ms].bitcast(FP8X4),
+                scales=wt_scales[:, t, k, ms],
+                in_=wt_grouped[:, t, k, ms].rearrange("p m j -> p (m j)"),
             )
 
-        for piece in range(PIECES):
-            wt_copies(piece)
-        w1_banks = w1_transposes(0)
-        wt_products()
-        w1_grouped = w1_copies(w1_banks)
+        def wt_product(t, k):
+            nc.tensor.matmul_mx(
+                out=up_banks[k][:, t * L : (t + 1) * L],
+                lhsT=wt_codes[:, t, k].bitcast(FP8X4),
+                lhsT_scale=wt_scales[:, t, k],
+                rhs=x_codes[:].bitcast(FP8X4),
+                rhs_scale=x_scales[:],
+                start=True,
+                stop=True,
+            )
 
         up_grouped = keep.tile([P, TAPS, L, PACK], BF16, align_bytes=64)
-        for k in range(TAPS):
+        up_codes = keep.tile([P, TAPS, L], U32, align_bytes=64)
+        up_scales = keep.tile([P, TAPS, L], U8, align_bytes=64)
+
+        def up_add(k):
             nc.vector.tensor_tensor(
                 out=up_grouped[:, k],
                 in0=up_banks[k][:].rearrange("p (j l) -> p l j", j=PACK),
                 in1=bt_col[:].unsqueeze(1).to_broadcast([P, L, PACK]),
                 op=ADD,
             )
-        w1_quantise(0, w1_grouped)
-        up_codes = keep.tile([P, T], U32, align_bytes=64)
-        up_scales = keep.tile([P, T], U8, align_bytes=64)
-        nc.vector.quantize_mx(
-            out=up_codes[:].bitcast(FP8X4),
-            scales=up_scales[:],
-            in_=up_grouped[:].rearrange("p k l j -> p (k l j)"),
-        )
 
-        for g in range(GROUPS):
-            for first in range(g * GROUP, (g + 1) * GROUP, STORE):
-                y_rows = results.tile([P, STORE, REPEATS * T], F32)
-                for i in range(STORE):
-                    n = first + i
-                    y_bank = sum_banks.tile([P, T], F32, tag="sums")
-                    nc.tensor.matmul_mx(
-                        out=y_bank[:],
-                        lhsT=w1_codes[:, n].bitcast(FP8X4),
-                        lhsT_scale=w1_scales[:, n],
-                        rhs=up_codes[:].bitcast(FP8X4),
-                        rhs_scale=up_scales[:],
-                        start=True,
-                        stop=True,
-                    )
-                    repeated = (
-                        y_bank[:]
-                        .rearrange("p (k l) -> p l k", k=TAPS)
-                        .unsqueeze(1)
-                        .to_broadcast([P, REPEATS, L, TAPS])
-                    )
-                    target = y_rows[:, i].rearrange("p (r l k) -> p r l k", r=REPEATS, k=TAPS)
-                    if i % 2 == 0:
-                        nc.scalar.activation(
-                            out=target, in_=repeated, func=IDENTITY, bias=b1_col[:, n : n + 1]
-                        )
-                    else:
-                        nc.vector.tensor_scalar(
-                            out=target, in0=repeated, scalar1=b1_col[:, n : n + 1], scalar2=None, op0=ADD
-                        )
-                nc.sync.dma_start(out=out[:, 0, first : first + STORE, :], in_=y_rows[:])
-                if first == g * GROUP and g + 1 < GROUPS:
-                    w1_grouped = w1_copies(w1_transposes(g + 1))
-            if g + 1 < GROUPS:
-                w1_quantise(g + 1, w1_grouped)
+        def up_quantise(k):
+            nc.vector.quantize_mx(
+                out=up_codes[:, k].bitcast(FP8X4),
+                scales=up_scales[:, k],
+                in_=up_grouped[:, k].rearrange("p l j -> p (l j)"),
+            )
+
+        w1_codes = keep.tile([P, LAYERS, P], U32, align_bytes=64)
+        w1_scales = keep.tile([P, LAYERS, P], U8, align_bytes=64)
+
+        per_bank = T // P
+
+        def w1_regroup(n0, layers, pair, w1_grouped):
+            w1_bank = word_banks.tile([P, T], F32, tag="words")
+            for f in range(per_bank):
+                s, u = divmod(pair * per_bank + f, HALVES)
+                nc.tensor.transpose(
+                    w1_bank[:, f * P : (f + 1) * P],
+                    w1_rows[:, n0 + s].bitcast(F32)[:, u : HALVES * P : HALVES],
+                    ident[:],
+                )
+            words = w1_grouped[:].bitcast(F32).rearrange("p (q f) -> p q f", f=layers * HALVES)
+            nc.scalar.copy(
+                out=words[:, :, pair * per_bank : (pair + 1) * per_bank],
+                in_=w1_bank[:].rearrange("p (f q) -> p q f", f=per_bank),
+            )
+
+        def w1_quantise(n0, layers, w1_grouped):
+            nc.vector.quantize_mx(
+                out=w1_codes[:, n0 : n0 + layers].rearrange("p n j -> p (n j)").bitcast(FP8X4),
+                scales=w1_scales[:, n0 : n0 + layers].rearrange("p n j -> p (n j)"),
+                in_=w1_grouped[:],
+            )
+
+        def w1_steps(n0, layers):
+            w1_grouped = stage.tile([P, layers * P * PACK], BF16, align_bytes=64)
+            steps = [partial(w1_regroup, n0, layers, pair, w1_grouped) for pair in range(layers // 2)]
+            steps.append(partial(w1_quantise, n0, layers, w1_grouped))
+            return steps
+
+        wt_copies(PIECES[0])
+        for k in range(TAPS):
+            for t in range(PACK):
+                wt_quantise(0, t, k)
+        nc.vector.tensor_copy(out=bias_rows[0:LAYERS, :], in_=b1_rows[:])
+        bias_bank = word_banks.tile([P, T], F32, tag="words")
+        nc.tensor.transpose(bias_bank[:, 0:P], bias_rows[:], ident[:])
+        b1_col = keep.tile([P, LAYERS], F32)
+        nc.vector.tensor_copy(out=b1_col[:], in_=bias_bank[:, 0:LAYERS])
+        bt_col = keep.tile([P, PACK], F32)
+        nc.vector.tensor_copy(out=bt_col[:], in_=bt_rows[:])
+
+        for piece in PIECES[1:]:
+            wt_copies(piece)
+        first_steps = w1_steps(0, GROUPS[0])
+        for step in first_steps[:-1]:
+            step()
+        for k in range(TAPS + 2):
+            if k < TAPS:
+                for t in range(PACK):
+                    wt_quantise(1, t, k)
+                    wt_product(t, k)
+            if 1 <= k <= TAPS:
+                up_add(k - 1)
+            if k >= 2:
+                up_quantise(k - 2)
+        first_steps[-1]()
+
+        def y_product(n):
+            y_bank = sum_banks.tile([P, T], F32, tag="sums")
+            nc.tensor.matmul_mx(
+                out=y_bank[:],
+                lhsT=w1_codes[:, n].bitcast(FP8X4),
+                lhsT_scale=w1_scales[:, n],
+                rhs=up_codes[:].rearrange("p k l -> p (k l)").bitcast(FP8X4),
+                rhs_scale=up_scales[:].rearrange("p k l -> p (k l)"),
+                start=True,
+                stop=True,
+            )
+            return y_bank[:].rearrange("p (k l) -> p l k", k=TAPS)
+
+        def y_copy(n, target, source):
+            if n % 2 == 0:
+                nc.scalar.activation(out=target, in_=source, func=IDENTITY, bias=b1_col[:, n : n + 1])
+            else:
+                nc.vector.tensor_scalar(
+                    out=target, in0=source, scalar1=b1_col[:, n : n + 1], scalar2=None, op0=ADD
+                )
+
+        def layer_once(n):
+            y_row = keep.tile([P, T], F32, tag="y_row", bufs=ONCE)
+            y_copy(n, y_row[:].rearrange("p (l k) -> p l k", k=TAPS), y_product(n))
+            nc.sync.dma_start(
+                out=out[:, 0, n, :].rearrange("j (r t) -> j r t", r=REPEATS),
+                in_=y_row[:].unsqueeze(1).to_broadcast([P, REPEATS, T]),
+            )
+
+        def layer(n, y_rows, i):
+            y_copy(
+                n,
+                y_rows[:, i].rearrange("p (r l k) -> p r l k", r=REPEATS, k=TAPS),
+                y_product(n).unsqueeze(1).to_broadcast([P, REPEATS, L, TAPS]),
+            )
+
+        y_rows = None
+        n0 = 0
+        for g, layers in enumerate(GROUPS):
+            steps = w1_steps(n0 + layers, GROUPS[g + 1]) if g + 1 < len(GROUPS) else []
+            for i in range(layers):
+                n = n0 + i
+                if n < ONCE:
+                    layer_once(n)
+                else:
+                    slot = (n - ONCE) % STORE
+                    if slot == 0:
+                        y_rows = results.tile([P, STORE, REPEATS * T], F32)
+                    layer(n, y_rows, slot)
+                    if slot == STORE - 1:
+                        nc.sync.dma_start(out=out[:, 0, n + 1 - STORE : n + 1, :], in_=y_rows[:])
+                for step in steps[i * len(steps) // layers : (i + 1) * len(steps) // layers]:
+                    step()
+            n0 += layers

@@ -22,7 +22,7 @@ T = L * TAPS
 LAYERS = 24
 REPEATS = 4
 WT_COLS = C * TAPS
-PIECES = ((0, 64), (64, 96), (96, 128))
+PIECES = ((0, 32), (32, 64), (64, 96), (96, 128))
 HALF = P // 2
 GROUPS = (2, 2, 4, 4, 4, 4, 4)
 ONCE = 2
@@ -49,8 +49,6 @@ def tile_conditionalfeaturesupsample_kernel(tc, local_features, wt, bt, w1, b1, 
         bt_rows = keep.tile([P, PACK], BF16)
 
         x_rows = keep.tile([P, C], BF16)
-        nc.sync.dma_start(out=x_rows[:], in_=local_features.rearrange("b l c -> (b l) c"))
-
         wt_rows = keep.tile([P, PACK, WT_COLS], BF16)
         wt_matrix = wt.rearrange("c o k -> c (o k)")
         m_cols = WT_COLS // P
@@ -61,6 +59,7 @@ def tile_conditionalfeaturesupsample_kernel(tc, local_features, wt, bt, w1, b1, 
                 in_=wt_matrix[:, cols].rearrange("(p j) w -> p j w", j=PACK),
             )
             if m0 == 0:
+                nc.sync.dma_start(out=x_rows[:], in_=local_features.rearrange("b l c -> (b l) c"))
                 nc.sync.dma_start(out=bt_rows[:], in_=bt.rearrange("(p t) -> p t", t=PACK))
                 nc.sync.dma_start(out=b1_rows[:], in_=b1.rearrange("(n j) -> n j", j=P))
 
@@ -127,6 +126,15 @@ def tile_conditionalfeaturesupsample_kernel(tc, local_features, wt, bt, w1, b1, 
         up_scales = keep.tile([P, TAPS, L], U8, align_bytes=64)
 
         def up_add(k):
+            if k == 0:
+                for t in range(PACK):
+                    nc.scalar.activation(
+                        out=up_grouped[:, k, :, t],
+                        in_=up_banks[k][:, t * L : (t + 1) * L],
+                        func=IDENTITY,
+                        bias=bt_col[:, t : t + 1],
+                    )
+                return
             nc.vector.tensor_tensor(
                 out=up_grouped[:, k],
                 in0=up_banks[k][:].rearrange("p (j l) -> p l j", j=PACK),
@@ -174,7 +182,8 @@ def tile_conditionalfeaturesupsample_kernel(tc, local_features, wt, bt, w1, b1, 
             steps.append(partial(w1_quantise, n0, layers, w1_grouped))
             return steps
 
-        wt_copies(PIECES[0])
+        for piece in PIECES[:2]:
+            wt_copies(piece)
         for k in range(TAPS):
             for t in range(PACK):
                 wt_quantise(0, t, k)
@@ -186,7 +195,7 @@ def tile_conditionalfeaturesupsample_kernel(tc, local_features, wt, bt, w1, b1, 
         bt_col = keep.tile([P, PACK], F32)
         nc.vector.tensor_copy(out=bt_col[:], in_=bt_rows[:])
 
-        for piece in PIECES[1:]:
+        for piece in PIECES[2:]:
             wt_copies(piece)
         first_steps = w1_steps(0, GROUPS[0])
         for step in first_steps[:-1]:

@@ -23,6 +23,8 @@ LAYERS = 24
 REPEATS = 4
 WT_COLS = C * TAPS
 PIECES = ((0, 32), (32, 64), (64, 96), (96, 128))
+SPANS = 2
+SPAN = L // SPANS
 HALF = P // 2
 GROUPS = (2, 2, 4, 4, 4, 4, 4)
 ONCE = 2
@@ -121,32 +123,32 @@ def tile_conditionalfeaturesupsample_kernel(tc, local_features, wt, bt, w1, b1, 
                 stop=True,
             )
 
-        up_grouped = keep.tile([P, TAPS, L, PACK], BF16, align_bytes=64)
-        up_codes = keep.tile([P, TAPS, L], U32, align_bytes=64)
-        up_scales = keep.tile([P, TAPS, L], U8, align_bytes=64)
+        up_grouped = keep.tile([P, SPANS, TAPS, SPAN, PACK], BF16, align_bytes=64)
+        up_codes = keep.tile([P, SPANS, TAPS * SPAN], U32, align_bytes=64)
+        up_scales = keep.tile([P, SPANS, TAPS * SPAN], U8, align_bytes=64)
 
-        def up_add(k):
+        def up_add(h, k):
             if k == 0:
                 for t in range(PACK):
                     nc.scalar.activation(
-                        out=up_grouped[:, k, :, t],
-                        in_=up_banks[k][:, t * L : (t + 1) * L],
+                        out=up_grouped[:, h, k, :, t],
+                        in_=up_banks[k][:, t * L + h * SPAN : t * L + (h + 1) * SPAN],
                         func=IDENTITY,
                         bias=bt_col[:, t : t + 1],
                     )
                 return
             nc.vector.tensor_tensor(
-                out=up_grouped[:, k],
-                in0=up_banks[k][:].rearrange("p (j l) -> p l j", j=PACK),
-                in1=bt_col[:].unsqueeze(1).to_broadcast([P, L, PACK]),
+                out=up_grouped[:, h, k],
+                in0=up_banks[k][:].rearrange("p (j l) -> p l j", j=PACK)[:, h * SPAN : (h + 1) * SPAN],
+                in1=bt_col[:].unsqueeze(1).to_broadcast([P, SPAN, PACK]),
                 op=ADD,
             )
 
-        def up_quantise(k):
+        def up_quantise(h):
             nc.vector.quantize_mx(
-                out=up_codes[:, k].bitcast(FP8X4),
-                scales=up_scales[:, k],
-                in_=up_grouped[:, k].rearrange("p l j -> p (l j)"),
+                out=up_codes[:, h].bitcast(FP8X4),
+                scales=up_scales[:, h],
+                in_=up_grouped[:, h].rearrange("p k l j -> p (k l j)"),
             )
 
         w1_codes = keep.tile([P, LAYERS, P], U32, align_bytes=64)
@@ -200,29 +202,30 @@ def tile_conditionalfeaturesupsample_kernel(tc, local_features, wt, bt, w1, b1, 
         first_steps = w1_steps(0, GROUPS[0])
         for step in first_steps[:-1]:
             step()
-        for k in range(TAPS + 2):
-            if k < TAPS:
-                for t in range(PACK):
-                    wt_quantise(1, t, k)
-                    wt_product(t, k)
-            if 1 <= k <= TAPS:
-                up_add(k - 1)
-            if k >= 2:
-                up_quantise(k - 2)
-        first_steps[-1]()
+        for k in range(TAPS):
+            for t in range(PACK):
+                wt_quantise(1, t, k)
+                wt_product(t, k)
+        for h in range(SPANS):
+            for k in range(TAPS):
+                up_add(h, k)
+            if h == 0:
+                first_steps[-1]()
+            up_quantise(h)
 
-        def y_product(n):
+        def y_product(n, h0, h1):
             y_bank = sum_banks.tile([P, T], F32, tag="sums")
+            cols = (h1 - h0) * TAPS * SPAN
             nc.tensor.matmul_mx(
-                out=y_bank[:],
+                out=y_bank[:, 0:cols],
                 lhsT=w1_codes[:, n].bitcast(FP8X4),
                 lhsT_scale=w1_scales[:, n],
-                rhs=up_codes[:].rearrange("p k l -> p (k l)").bitcast(FP8X4),
-                rhs_scale=up_scales[:].rearrange("p k l -> p (k l)"),
+                rhs=up_codes[:, h0:h1].rearrange("p h c -> p (h c)").bitcast(FP8X4),
+                rhs_scale=up_scales[:, h0:h1].rearrange("p h c -> p (h c)"),
                 start=True,
                 stop=True,
             )
-            return y_bank[:].rearrange("p (k l) -> p l k", k=TAPS)
+            return y_bank[:, 0:cols].rearrange("p (h k l) -> p h l k", k=TAPS, l=SPAN)
 
         def y_copy(n, target, source):
             if n % 2 == 0:
@@ -232,20 +235,28 @@ def tile_conditionalfeaturesupsample_kernel(tc, local_features, wt, bt, w1, b1, 
                     out=target, in0=source, scalar1=b1_col[:, n : n + 1], scalar2=None, op0=ADD
                 )
 
-        def layer_once(n):
-            y_row = keep.tile([P, T], F32, tag="y_row", bufs=ONCE)
-            y_copy(n, y_row[:].rearrange("p (l k) -> p l k", k=TAPS), y_product(n))
+        def layer_once(n, h0, h1):
+            cols = (h1 - h0) * TAPS * SPAN
+            y_row = keep.tile([P, T], F32, tag="y_row", bufs=ONCE + SPANS)
+            y_copy(
+                n,
+                y_row[:, 0:cols].rearrange("p (h l k) -> p h l k", l=SPAN, k=TAPS),
+                y_product(n, h0, h1),
+            )
             nc.sync.dma_start(
-                out=out[:, 0, n, :].rearrange("j (r t) -> j r t", r=REPEATS),
-                in_=y_row[:].unsqueeze(1).to_broadcast([P, REPEATS, T]),
+                out=out[:, 0, n, :].rearrange("j (r t) -> j r t", r=REPEATS)[
+                    :, :, h0 * TAPS * SPAN : h1 * TAPS * SPAN
+                ],
+                in_=y_row[:, 0:cols].unsqueeze(1).to_broadcast([P, REPEATS, cols]),
             )
 
         def layer(n, y_rows, i):
-            y_copy(
-                n,
-                y_rows[:, i].rearrange("p (r l k) -> p r l k", r=REPEATS, k=TAPS),
-                y_product(n).unsqueeze(1).to_broadcast([P, REPEATS, L, TAPS]),
-            )
+            source = y_product(n, 0, SPANS)
+            target = y_rows[:, i].rearrange("p (r h l k) -> p h r l k", r=REPEATS, l=SPAN, k=TAPS)
+            for h in range(SPANS):
+                y_copy(
+                    n, target[:, h], source[:, h].unsqueeze(1).to_broadcast([P, REPEATS, SPAN, TAPS])
+                )
 
         y_rows = None
         n0 = 0
@@ -253,8 +264,11 @@ def tile_conditionalfeaturesupsample_kernel(tc, local_features, wt, bt, w1, b1, 
             steps = w1_steps(n0 + layers, GROUPS[g + 1]) if g + 1 < len(GROUPS) else []
             for i in range(layers):
                 n = n0 + i
-                if n < ONCE:
-                    layer_once(n)
+                if n == 0:
+                    for h in range(SPANS):
+                        layer_once(n, h, h + 1)
+                elif n < ONCE:
+                    layer_once(n, 0, SPANS)
                 else:
                     slot = (n - ONCE) % STORE
                     if slot == 0:

@@ -28,7 +28,7 @@ SPAN = L // SPANS
 HALF = P // 2
 GROUPS = (2, 2, 4, 4, 4, 4, 4)
 ONCE = 2
-STORE = 2
+STORES = (2, 2, 4, 4, 4, 4, 2)
 
 FLOPS = 2 * L * C * WT_COLS + 2 * LAYERS * P * C * T
 
@@ -38,7 +38,7 @@ def tile_conditionalfeaturesupsample_kernel(tc, local_features, wt, bt, w1, b1, 
     with ExitStack() as ctx:
         keep = ctx.enter_context(tc.tile_pool(name="keep", bufs=1))
         stage = ctx.enter_context(tc.tile_pool(name="stage", bufs=2))
-        results = ctx.enter_context(tc.tile_pool(name="results", bufs=4))
+        results = ctx.enter_context(tc.tile_pool(name="results", bufs=3))
         word_banks = ctx.enter_context(tc.psum_pool(name="word_banks", bufs=3))
         sum_banks = ctx.enter_context(tc.psum_pool(name="sum_banks", bufs=5))
 
@@ -258,6 +258,13 @@ def tile_conditionalfeaturesupsample_kernel(tc, local_features, wt, bt, w1, b1, 
                     n, target[:, h], source[:, h].unsqueeze(1).to_broadcast([P, REPEATS, SPAN, TAPS])
                 )
 
+        store_of = {}
+        first = ONCE
+        for i, count in enumerate(STORES):
+            for slot in range(count):
+                store_of[first + slot] = (first, count, nc.scalar if i % 2 else nc.sync)
+            first += count
+
         y_rows = None
         n0 = 0
         for g, layers in enumerate(GROUPS):
@@ -270,12 +277,12 @@ def tile_conditionalfeaturesupsample_kernel(tc, local_features, wt, bt, w1, b1, 
                 elif n < ONCE:
                     layer_once(n, 0, SPANS)
                 else:
-                    slot = (n - ONCE) % STORE
-                    if slot == 0:
-                        y_rows = results.tile([P, STORE, REPEATS * T], F32)
-                    layer(n, y_rows, slot)
-                    if slot == STORE - 1:
-                        nc.sync.dma_start(out=out[:, 0, n + 1 - STORE : n + 1, :], in_=y_rows[:])
+                    first, count, queue = store_of[n]
+                    if n == first:
+                        y_rows = results.tile([P, count, REPEATS * T], F32)
+                    layer(n, y_rows, n - first)
+                    if n == first + count - 1:
+                        queue.dma_start(out=out[:, 0, first : first + count, :], in_=y_rows[:])
                 for step in steps[i * len(steps) // layers : (i + 1) * len(steps) // layers]:
                     step()
             n0 += layers

from contextlib import ExitStack
from functools import partial

import concourse.mybir as mybir
from concourse.masks import make_identity

BF16 = mybir.dt.bfloat16
F32 = mybir.dt.float32
U32 = mybir.dt.uint32
U8 = mybir.dt.uint8
FP8X4 = mybir.dt.float8_e4m3fn_x4
ADD = mybir.AluOpType.add
IDENTITY = mybir.ActivationFunctionType.Identity

P = 128
PACK = 4
HALVES = 2
L = 128
C = 512
TAPS = 4
T = L * TAPS
LAYERS = 24
REPEATS = 4
WT_COLS = C * TAPS
PIECES = ((0, 32), (32, 64), (64, 96), (96, 128))
SPANS = 2
SPAN = L // SPANS
HALF = P // 2
GROUPS = (2, 2, 4, 4, 4, 4, 4)
ONCE = 2
STORES = (2, 2, 4, 4, 4, 4, 2)

FLOPS = 2 * L * C * WT_COLS + 2 * LAYERS * P * C * T


def tile_conditionalfeaturesupsample_kernel(tc, local_features, wt, bt, w1, b1, out):
    nc = tc.nc
    with ExitStack() as ctx:
        keep = ctx.enter_context(tc.tile_pool(name="keep", bufs=1))
        stage = ctx.enter_context(tc.tile_pool(name="stage", bufs=2))
        results = ctx.enter_context(tc.tile_pool(name="results", bufs=3))
        word_banks = ctx.enter_context(tc.psum_pool(name="word_banks", bufs=3))
        sum_banks = ctx.enter_context(tc.psum_pool(name="sum_banks", bufs=5))

        ident = keep.tile([P, P], F32)
        make_identity(nc, ident[:])

        bias_rows = keep.tile([P, P], F32)
        nc.vector.memset(bias_rows[:], 0.0)
        b1_rows = keep.tile([LAYERS, P], BF16)
        bt_rows = keep.tile([P, PACK], BF16)

        x_rows = keep.tile([P, C], BF16)
        wt_rows = keep.tile([P, PACK, WT_COLS], BF16)
        wt_matrix = wt.rearrange("c o k -> c (o k)")
        m_cols = WT_COLS // P
        for m0, m1 in PIECES:
            cols = slice(m0 * m_cols, m1 * m_cols)
            nc.sync.dma_start(
                out=wt_rows[:, :, cols],
                in_=wt_matrix[:, cols].rearrange("(p j) w -> p j w", j=PACK),
            )
            if m0 == 0:
                nc.sync.dma_start(out=x_rows[:], in_=local_features.rearrange("b l c -> (b l) c"))
                nc.sync.dma_start(out=bt_rows[:], in_=bt.rearrange("(p t) -> p t", t=PACK))
                nc.sync.dma_start(out=b1_rows[:], in_=b1.rearrange("(n j) -> n j", j=P))

        w1_rows = keep.tile([P, LAYERS, C], BF16)
        n0 = 0
        for layers in GROUPS:
            nc.sync.dma_start(
                out=w1_rows[:, n0 : n0 + layers],
                in_=w1[n0 * P : (n0 + layers) * P, :].rearrange("(q s) c -> q s c", s=layers),
            )
            n0 += layers

        x_bank = word_banks.tile([P, T], F32, tag="words")
        for u in range(HALVES):
            nc.tensor.transpose(
                x_bank[:, u * P : (u + 1) * P], x_rows[:].bitcast(F32)[:, u : HALVES * P : HALVES], ident[:]
            )
        x_grouped = keep.tile([P, L * PACK], BF16, align_bytes=64)
        nc.vector.tensor_copy(
            out=x_grouped[:].bitcast(F32).rearrange("p (l u) -> p l u", u=HALVES),
            in_=x_bank[:, 0 : HALVES * P].rearrange("p (u l) -> p l u", u=HALVES),
        )
        x_codes = keep.tile([P, L], U32, align_bytes=64)
        x_scales = keep.tile([P, L], U8, align_bytes=64)
        nc.vector.quantize_mx(out=x_codes[:].bitcast(FP8X4), scales=x_scales[:], in_=x_grouped[:])

        wt_grouped = keep.tile([P, PACK, TAPS, P, PACK], BF16, align_bytes=64)
        wt_codes = keep.tile([P, PACK, TAPS, P], U32, align_bytes=64)
        wt_scales = keep.tile([P, PACK, TAPS, P], U8, align_bytes=64)
        wt_sorted = wt_rows[:].rearrange("p j (m t k) -> p t m j k", t=PACK, k=TAPS)
        wt_targets = wt_grouped[:].rearrange("p t k m j -> p t m j k")
        up_banks = []
        for k in range(TAPS):
            up_bank = sum_banks.tile([P, T], F32, tag="sums")
            up_banks.append(up_bank)

        def wt_copies(piece):
            ms = slice(piece[0], piece[1])
            for t in range(PACK // 2):
                nc.vector.tensor_copy(out=wt_targets[:, t, ms], in_=wt_sorted[:, t, ms])
                nc.scalar.copy(out=wt_targets[:, t + 2, ms], in_=wt_sorted[:, t + 2, ms])

        def wt_quantise(h, t, k):
            ms = slice(h * HALF, (h + 1) * HALF)
            nc.vector.quantize_mx(
                out=wt_codes[:, t, k, ms].bitcast(FP8X4),
                scales=wt_scales[:, t, k, ms],
                in_=wt_grouped[:, t, k, ms].rearrange("p m j -> p (m j)"),
            )

        def wt_product(t, k):
            nc.tensor.matmul_mx(
                out=up_banks[k][:, t * L : (t + 1) * L],
                lhsT=wt_codes[:, t, k].bitcast(FP8X4),
                lhsT_scale=wt_scales[:, t, k],
                rhs=x_codes[:].bitcast(FP8X4),
                rhs_scale=x_scales[:],
                start=True,
                stop=True,
            )

        up_grouped = keep.tile([P, SPANS, TAPS, SPAN, PACK], BF16, align_bytes=64)
        up_codes = keep.tile([P, SPANS, TAPS * SPAN], U32, align_bytes=64)
        up_scales = keep.tile([P, SPANS, TAPS * SPAN], U8, align_bytes=64)

        def up_add(h, k):
            if k == 0:
                for t in range(PACK):
                    nc.scalar.activation(
                        out=up_grouped[:, h, k, :, t],
                        in_=up_banks[k][:, t * L + h * SPAN : t * L + (h + 1) * SPAN],
                        func=IDENTITY,
                        bias=bt_col[:, t : t + 1],
                    )
                return
            nc.vector.tensor_tensor(
                out=up_grouped[:, h, k],
                in0=up_banks[k][:].rearrange("p (j l) -> p l j", j=PACK)[:, h * SPAN : (h + 1) * SPAN],
                in1=bt_col[:].unsqueeze(1).to_broadcast([P, SPAN, PACK]),
                op=ADD,
            )

        def up_quantise(h):
            nc.vector.quantize_mx(
                out=up_codes[:, h].bitcast(FP8X4),
                scales=up_scales[:, h],
                in_=up_grouped[:, h].rearrange("p k l j -> p (k l j)"),
            )

        w1_codes = keep.tile([P, LAYERS, P], U32, align_bytes=64)
        w1_scales = keep.tile([P, LAYERS, P], U8, align_bytes=64)

        per_bank = T // P

        def w1_regroup(n0, layers, pair, w1_grouped):
            w1_bank = word_banks.tile([P, T], F32, tag="words")
            for f in range(per_bank):
                s, u = divmod(pair * per_bank + f, HALVES)
                nc.tensor.transpose(
                    w1_bank[:, f * P : (f + 1) * P],
                    w1_rows[:, n0 + s].bitcast(F32)[:, u : HALVES * P : HALVES],
                    ident[:],
                )
            words = w1_grouped[:].bitcast(F32).rearrange("p (q f) -> p q f", f=layers * HALVES)
            nc.scalar.copy(
                out=words[:, :, pair * per_bank : (pair + 1) * per_bank],
                in_=w1_bank[:].rearrange("p (f q) -> p q f", f=per_bank),
            )

        def w1_quantise(n0, layers, w1_grouped):
            nc.vector.quantize_mx(
                out=w1_codes[:, n0 : n0 + layers].rearrange("p n j -> p (n j)").bitcast(FP8X4),
                scales=w1_scales[:, n0 : n0 + layers].rearrange("p n j -> p (n j)"),
                in_=w1_grouped[:],
            )

        def w1_steps(n0, layers):
            w1_grouped = stage.tile([P, layers * P * PACK], BF16, align_bytes=64)
            steps = [partial(w1_regroup, n0, layers, pair, w1_grouped) for pair in range(layers // 2)]
            steps.append(partial(w1_quantise, n0, layers, w1_grouped))
            return steps

        for piece in PIECES[:2]:
            wt_copies(piece)
        for k in range(TAPS):
            for t in range(PACK):
                wt_quantise(0, t, k)
        nc.vector.tensor_copy(out=bias_rows[0:LAYERS, :], in_=b1_rows[:])
        bias_bank = word_banks.tile([P, T], F32, tag="words")
        nc.tensor.transpose(bias_bank[:, 0:P], bias_rows[:], ident[:])
        b1_col = keep.tile([P, LAYERS], F32)
        nc.vector.tensor_copy(out=b1_col[:], in_=bias_bank[:, 0:LAYERS])
        bt_col = keep.tile([P, PACK], F32)
        nc.vector.tensor_copy(out=bt_col[:], in_=bt_rows[:])

        for piece in PIECES[2:]:
            wt_copies(piece)
        first_steps = w1_steps(0, GROUPS[0])
        for step in first_steps[:-1]:
            step()
        for k in range(TAPS):
            for t in range(PACK):
                wt_quantise(1, t, k)
                wt_product(t, k)
        for h in range(SPANS):
            for k in range(TAPS):
                up_add(h, k)
            if h == 0:
                first_steps[-1]()
            up_quantise(h)

        def y_product(n, h0, h1):
            y_bank = sum_banks.tile([P, T], F32, tag="sums")
            cols = (h1 - h0) * TAPS * SPAN
            nc.tensor.matmul_mx(
                out=y_bank[:, 0:cols],
                lhsT=w1_codes[:, n].bitcast(FP8X4),
                lhsT_scale=w1_scales[:, n],
                rhs=up_codes[:, h0:h1].rearrange("p h c -> p (h c)").bitcast(FP8X4),
                rhs_scale=up_scales[:, h0:h1].rearrange("p h c -> p (h c)"),
                start=True,
                stop=True,
            )
            return y_bank[:, 0:cols].rearrange("p (h k l) -> p h l k", k=TAPS, l=SPAN)

        def y_copy(n, target, source):
            if n % 2 == 0:
                nc.scalar.activation(out=target, in_=source, func=IDENTITY, bias=b1_col[:, n : n + 1])
            else:
                nc.vector.tensor_scalar(
                    out=target, in0=source, scalar1=b1_col[:, n : n + 1], scalar2=None, op0=ADD
                )

        def layer_once(n, h0, h1):
            cols = (h1 - h0) * TAPS * SPAN
            y_row = keep.tile([P, T], F32, tag="y_row", bufs=ONCE + SPANS)
            y_copy(
                n,
                y_row[:, 0:cols].rearrange("p (h l k) -> p h l k", l=SPAN, k=TAPS),
                y_product(n, h0, h1),
            )
            nc.sync.dma_start(
                out=out[:, 0, n, :].rearrange("j (r t) -> j r t", r=REPEATS)[
                    :, :, h0 * TAPS * SPAN : h1 * TAPS * SPAN
                ],
                in_=y_row[:, 0:cols].unsqueeze(1).to_broadcast([P, REPEATS, cols]),
            )

        def layer(n, y_rows, i):
            source = y_product(n, 0, SPANS)
            target = y_rows[:, i].rearrange("p (r h l k) -> p h r l k", r=REPEATS, l=SPAN, k=TAPS)
            for h in range(SPANS):
                y_copy(
                    n, target[:, h], source[:, h].unsqueeze(1).to_broadcast([P, REPEATS, SPAN, TAPS])
                )

        store_of = {}
        first = ONCE
        for i, count in enumerate(STORES):
            for slot in range(count):
                store_of[first + slot] = (first, count, nc.scalar if i % 2 else nc.sync)
            first += count

        y_rows = None
        n0 = 0
        for g, layers in enumerate(GROUPS):
            steps = w1_steps(n0 + layers, GROUPS[g + 1]) if g + 1 < len(GROUPS) else []
            for i in range(layers):
                n = n0 + i
                if n == 0:
                    for h in range(SPANS):
                        layer_once(n, h, h + 1)
                elif n < ONCE:
                    layer_once(n, 0, SPANS)
                else:
                    first, count, queue = store_of[n]
                    if n == first:
                        y_rows = results.tile([P, count, REPEATS * T], F32)
                    layer(n, y_rows, n - first)
                    if n == first + count - 1:
                        queue.dma_start(out=out[:, 0, first : first + count, :], in_=y_rows[:])
                for step in steps[i * len(steps) // layers : (i + 1) * len(steps) // layers]:
                    step()
            n0 += layers
